import numpy as np
import ml_dtypes


def mxq(x, axis, fmt="e4m3"):
    dtype, down = {"e4m3": (ml_dtypes.float8_e4m3fn, 7), "e5m2": (ml_dtypes.float8_e5m2, 14)}[fmt]
    v = np.moveaxis(np.asarray(x, np.float32).astype(ml_dtypes.bfloat16).astype(np.float64), axis, -1)
    blocks = v.reshape(v.shape[:-1] + (-1, 32))
    amax = np.abs(blocks).max(-1, keepdims=True)
    byte = np.maximum(np.where(amax > 0, np.frexp(amax)[1] - 1 + 127, 0) - down, 1)
    scale = np.exp2(byte - 127.0)
    codes = (blocks / scale).astype(np.float32).astype(dtype).astype(np.float64)
    return np.moveaxis((codes * scale).reshape(v.shape), -1, axis)


WIDE = False


def mx_kscale(k):
    if not WIDE:
        return np.ones(k)
    levels = np.array([10, -10, 5, -5, 0])
    a = np.random.permutation(np.resize(levels, k // 512 * 4)).reshape(k // 512, 4)
    idx = np.arange(k)
    return np.exp2(a[idx // 512, idx % 128 // 32])


BF16 = ml_dtypes.bfloat16


def bf(x):
    return np.asarray(x, np.float32).astype(BF16)


def f64(x):
    return np.asarray(x).astype(np.float64)


B, K, N, F = 8, 2, 512, 512


def sigmoid(v):
    return 1.0 / (1.0 + np.exp(-v))


def setup_inputs():
    t = mx_kscale(K * F)[:F]
    return {"H": bf(np.random.standard_normal((B, N, F)) * t),
            "E": bf(np.random.random((B, K, N, N)) * 10.0 / N),
            "RW": bf(np.random.standard_normal((F, F, K)) * 0.7 * np.sqrt(K * N / F) / t[:, None, None]),
            "SW": bf(np.random.standard_normal((F, F)) / np.sqrt(F) / t[:, None])}


def reference(H, E, RW, SW):
    Hf, Ef = f64(H), f64(E)
    n = Ef.shape[2]
    D = 1.0 / (Ef + np.eye(n)).sum(axis=(1, 2))
    G = mxq(Ef, 3, "e4m3") @ mxq(Hf, 1, "e4m3")[:, None]
    X = G.transpose(0, 2, 1, 3).reshape(B, N, K * F)
    W = f64(RW).transpose(2, 0, 1).reshape(K * F, F)
    rel = mxq(X, 2, "e4m3") @ mxq(W, 0, "e4m3")
    self_term = Hf @ f64(SW)
    return sigmoid(D[:, :, None] * rel + self_term)

@@ -1,0 +1,303 @@
+from contextlib import ExitStack
+
+import concourse.mybir as mybir
+from concourse.masks import make_identity
+
+F32 = mybir.dt.float32
+BF16 = mybir.dt.bfloat16
+U32 = mybir.dt.uint32
+U8 = mybir.dt.uint8
+FP8X4 = mybir.dt.float8_e4m3fn_x4
+ACT = mybir.ActivationFunctionType
+ALU = mybir.AluOpType
+
+P = 128
+B = 8
+K = 2
+N = 512
+F = 512
+FLOPS = 2 * B * K * N * N * F + 2 * B * N * K * F * F + 2 * B * N * F * F
+
+ET_EXIT = ("v", "v", "v", "s")
+HT_EXIT = ("s", "s")
+G_EXIT = ("s", "v", "s", "s", "v", "s", "v", "s")
+
+
+def tile_rgcnconv_t_kernel(tc, H, E, RW, SW, out):
+    nc = tc.nc
+    with ExitStack() as ctx:
+        const = ctx.enter_context(tc.tile_pool(name="const", bufs=1))
+        inp = ctx.enter_context(tc.tile_pool(name="inp", bufs=3))
+        work = ctx.enter_context(tc.tile_pool(name="work", bufs=2))
+        psum = ctx.enter_context(tc.psum_pool(name="psum", bufs=8))
+
+        st = {}
+
+        def bank(name):
+            return psum.tile([P, 512], F32, name=name, tag="bank")
+
+        def evac(eng, dst, src):
+            if eng == "v":
+                nc.vector.tensor_copy(out=dst, in_=src)
+            else:
+                nc.scalar.copy(out=dst, in_=src)
+
+        def load_e(b):
+            enat = inp.tile([P, K, 4, N], BF16, name="enat%d" % b, tag="enat")
+            st[("enat", b)] = enat
+            for k in range(K):
+                nc.sync.dma_start(out=enat[:, k], in_=E[b, k].rearrange("(c p) j -> p c j", p=P))
+
+        def load_h(b):
+            ha = inp.tile([P, 4 * F], BF16, name="ha%d" % b, tag="ha")
+            st[("ha", b)] = ha
+            nc.sync.dma_start(
+                out=ha[:].rearrange("p (u x) -> p u x", u=2),
+                in_=H[b].rearrange("(u p e) m -> p u (e m)", u=2, e=2),
+            )
+            hb = inp.tile([P, 4, F], BF16, name="hb%d" % b, tag="hb")
+            st[("hb", b)] = hb
+            nc.sync.dma_start(out=hb[:], in_=H[b].rearrange("(c p) m -> p c m", p=P))
+
+        load_e(0)
+        load_h(0)
+        rw_raw = const.tile([P, 4, F * K], BF16, name="rw_raw")
+        nc.sync.dma_start(out=rw_raw[:], in_=RW.rearrange("(t p) f k -> p t (f k)", p=P))
+        sw_sb = const.tile([P, 2, 2, F], BF16, name="sw_sb")
+        nc.sync.dma_start(
+            out=sw_sb[:].rearrange("w u e f -> w u (e f)"),
+            in_=SW.rearrange("(u w e) f -> w u (e f)", u=2, e=2),
+        )
+        load_e(1)
+        load_h(1)
+
+        ident = const.tile([P, P], F32, name="ident")
+        make_identity(nc, ident[:])
+        ones = const.tile([P, 32], BF16, name="ones")
+        nc.vector.memset(ones[:], 1.0)
+
+        w_grp = const.tile([P, K, 4 * F], BF16, name="w_grp", align_bytes=64)
+        w_codes = const.tile([P, K, F], U32, name="w_codes", align_bytes=64)
+        w_scales = const.tile([P, K, F], U8, name="w_scales", align_bytes=64)
+
+        def quantise_w():
+            src = rw_raw[:].rearrange("p t (f k) -> p k f t", k=K)
+            for k in range(K):
+                evac("vs"[k], w_grp[:, k, :].rearrange("p (f t) -> p f t", t=4), src[:, k])
+            for k in range(K):
+                nc.vector.quantize_mx(
+                    out=w_codes[:, k, :].bitcast(FP8X4), scales=w_scales[:, k, :], in_=w_grp[:, k, :]
+                )
+
+        def quantise_h(b):
+            ha = st[("ha", b)]
+            hgr = work.tile([P, 4 * F], BF16, name="hgr%d" % b, tag="hgr", align_bytes=64)
+            nc.vector.tensor_copy(
+                out=hgr[:].rearrange("p (c i t) -> p c t i", i=4, t=4),
+                in_=ha[:].rearrange("p (t c i) -> p c t i", t=4, i=4),
+            )
+            hc = work.tile([P, F], U32, name="hc%d" % b, tag="hc", align_bytes=64)
+            hs = work.tile([P, F], U8, name="hs%d" % b, tag="hs", align_bytes=64)
+            nc.vector.quantize_mx(out=hc[:].bitcast(FP8X4), scales=hs[:], in_=hgr[:])
+            st[("hc", b)] = hc
+            st[("hs", b)] = hs
+
+        def et_op(b, k, h, u, cc):
+            if u == 0 and cc == 0:
+                st["tr"] = bank("tre%d_%d_%d" % (b, k, h))
+                if h == 0:
+                    st[("egr", b, k)] = work.tile(
+                        [P, 4 * N], BF16, name="egr%d_%d" % (b, k), tag="egr", bufs=3, align_bytes=64
+                    )
+            tr = st["tr"]
+            enat = st[("enat", b)]
+            nc.tensor.transpose(
+                tr[:, 256 * u + 128 * cc : 256 * u + 128 * cc + 128],
+                enat[:, k, 2 * h + cc, :].bitcast(F32)[:, 128 * u : 128 * u + 128],
+                ident[:],
+            )
+            if u == 1 and cc == 1:
+                egr = st[("egr", b, k)]
+                evac(
+                    ET_EXIT[2 * k + h],
+                    egr[:].bitcast(F32).rearrange("p (i u) -> p i u", u=2)[:, 256 * h : 256 * h + 256, :],
+                    tr[:].rearrange("p (u i) -> p i u", u=2),
+                )
+                if h == 1:
+                    ec = work.tile([P, N], U32, name="ec%d_%d" % (b, k), tag="ec", bufs=4, align_bytes=64)
+                    es = work.tile([P, N], U8, name="es%d_%d" % (b, k), tag="es", bufs=4, align_bytes=64)
+                    nc.vector.quantize_mx(out=ec[:].bitcast(FP8X4), scales=es[:], in_=egr[:])
+                    st[("ec", b, k)] = ec
+                    st[("es", b, k)] = es
+
+        def ht_op(b, u, c):
+            if c == 0:
+                st["tr"] = bank("trh%d_%d" % (b, u))
+                if u == 0:
+                    st[("ht", b)] = work.tile([P, 2, N, 2], BF16, name="ht%d" % b, tag="ht")
+            tr = st["tr"]
+            hb = st[("hb", b)]
+            nc.tensor.transpose(
+                tr[:, 128 * c : 128 * c + 128],
+                hb[:, c, :].bitcast(F32)[:, 128 * u : 128 * u + 128],
+                ident[:],
+            )
+            if c == 3:
+                ht = st[("ht", b)]
+                evac(HT_EXIT[u], ht[:, u].rearrange("p n e -> p (n e)").bitcast(F32), tr[:])
+
+        def d_op(b, c, k, c2):
+            if c == 0 and k == 0 and c2 == 0:
+                st["dp"] = bank("dp%d" % b)
+            dp = st["dp"]
+            enat = st[("enat", b)]
+            nc.tensor.matmul(
+                dp[:, 32 * c : 32 * c + 32],
+                lhsT=enat[:, k, c2, 128 * c : 128 * c + 128],
+                rhs=ones[:],
+                start=(k == 0 and c2 == 0),
+                stop=(k == K - 1 and c2 == 3),
+            )
+            if c == 3 and k == K - 1 and c2 == 3:
+                dsum = work.tile([P, 4], F32, name="dsum%d" % b, tag="dsum")
+                nc.vector.tensor_scalar_add(
+                    out=dsum[:], in0=dp[:, 0:128].rearrange("p (c n) -> p c n", n=32)[:, :, 0], scalar1=2.0
+                )
+                dinv = work.tile([P, 4], F32, name="dinv%d" % b, tag="dinv", bufs=3)
+                nc.vector.reciprocal(out=dinv[:], in_=dsum[:])
+                st[("dinv", b)] = dinv
+
+        def side_ops(b):
+            trs = []
+            for k in range(K):
+                for h in range(2):
+                    for u in range(2):
+                        for cc in range(2):
+                            trs.append(lambda k=k, h=h, u=u, cc=cc: et_op(b, k, h, u, cc))
+            for u in range(2):
+                for c in range(4):
+                    trs.append(lambda u=u, c=c: ht_op(b, u, c))
+            ds = []
+            for c in range(4):
+                for k in range(K):
+                    for c2 in range(4):
+                        ds.append(lambda c=c, k=k, c2=c2: d_op(b, c, k, c2))
+            return merge(trs, ds)
+
+        def merge(main, side):
+            res = []
+            done = 0
+            for idx in range(len(main)):
+                res.append(main[idx])
+                want = (idx + 1) * len(side) // len(main)
+                res.extend(side[done:want])
+                done = want
+            return res
+
+        def self_op(b, c, q):
+            if q == 0:
+                st["sp"] = bank("sp%d_%d" % (b, c))
+            sp = st["sp"]
+            ht = st[("ht", b)]
+            u = q // 2
+            e = q % 2
+            nc.tensor.matmul(
+                sp[:],
+                lhsT=ht[:, u, 128 * c : 128 * c + 128, e],
+                rhs=sw_sb[:, u, e, :],
+                start=(q == 0),
+                stop=(q == 3),
+            )
+            if q == 3:
+                ssb = work.tile([P, F], F32, name="ssb%d_%d" % (b, c), tag="ssb", bufs=6)
+                nc.scalar.copy(out=ssb[:], in_=sp[:])
+                st[("ssb", b, c)] = ssb
+
+        def self_ops(b):
+            ops = []
+            for c in range(4):
+                for q in range(4):
+                    ops.append(lambda c=c, q=q: self_op(b, c, q))
+            return ops
+
+        def stage1(b):
+            hc = st[("hc", b)]
+            hs = st[("hs", b)]
+            xgr = work.tile([P, K, 4 * N], BF16, name="xgr%d" % b, tag="xgr", align_bytes=64)
+            xc = work.tile([P, K, N], U32, name="xc%d" % b, tag="xc", align_bytes=64)
+            xs = work.tile([P, K, N], U8, name="xs%d" % b, tag="xs", align_bytes=64)
+            st[("xc", b)] = xc
+            st[("xs", b)] = xs
+            for k in range(K):
+                ec = st[("ec", b, k)]
+                es = st[("es", b, k)]
+                for ib in range(4):
+                    g = bank("g%d_%d_%d" % (b, k, ib))
+                    for t in range(4):
+                        nc.tensor.matmul_mx(
+                            out=g[:, 128 * t : 128 * t + 128],
+                            lhsT=hc[:, 128 * t : 128 * t + 128].bitcast(FP8X4),
+                            lhsT_scale=hs[:, 128 * t : 128 * t + 128],
+                            rhs=ec[:, 128 * ib : 128 * ib + 128].bitcast(FP8X4),
+                            rhs_scale=es[:, 128 * ib : 128 * ib + 128],
+                            start=True,
+                            stop=True,
+                        )
+                    evac(
+                        G_EXIT[4 * k + ib],
+                        xgr[:, k, :].rearrange("p (i t) -> p i t", t=4)[:, 128 * ib : 128 * ib + 128, :],
+                        g[:].rearrange("p (t i) -> p i t", t=4),
+                    )
+                nc.vector.quantize_mx(out=xc[:, k, :].bitcast(FP8X4), scales=xs[:, k, :], in_=xgr[:, k, :])
+
+        def stage2(b):
+            xc = st[("xc", b)]
+            xs = st[("xs", b)]
+            dinv = st[("dinv", b)]
+            y = work.tile([P, 4, F], F32, name="y%d" % b, tag="y")
+            for c in range(4):
+                r = bank("r%d_%d" % (b, c))
+                for k in range(K):
+                    nc.tensor.matmul_mx(
+                        out=r[:],
+                        lhsT=xc[:, k, 128 * c : 128 * c + 128].bitcast(FP8X4),
+                        lhsT_scale=xs[:, k, 128 * c : 128 * c + 128],
+                        rhs=w_codes[:, k, :].bitcast(FP8X4),
+                        rhs_scale=w_scales[:, k, :],
+                        start=(k == 0),
+                        stop=(k == K - 1),
+                    )
+                nc.vector.scalar_tensor_tensor(
+                    out=y[:, c, :],
+                    in0=r[:],
+                    scalar=dinv[:, c : c + 1],
+                    in1=st[("ssb", b, c)][:],
+                    op0=ALU.mult,
+                    op1=ALU.add,
+                )
+                nc.scalar.activation(out=y[:, c, :], in_=y[:, c, :], func=ACT.Sigmoid)
+                if c % 2 == 1:
+                    nc.sync.dma_start(
+                        out=out[b].rearrange("(c p) f -> p c f", p=P)[:, c - 1 : c + 1, :],
+                        in_=y[:, c - 1 : c + 1, :],
+                    )
+
+        quantise_h(0)
+        for op in side_ops(0):
+            op()
+        quantise_w()
+        stage1(0)
+        for b in range(B):
+            if b + 2 < B:
+                load_e(b + 2)
+                load_h(b + 2)
+            if b + 1 < B:
+                quantise_h(b + 1)
+                for op in merge(self_ops(b), side_ops(b + 1)):
+                    op()
+            else:
+                for op in self_ops(b):
+                    op()
+            stage2(b)
+            if b + 1 < B:
+                stage1(b + 1)

@@ -18,9 +18,11 @@ N = 512
 F = 512
 FLOPS = 2 * B * K * N * N * F + 2 * B * N * K * F * F + 2 * B * N * F * F
 
-ET_EXIT = ("v", "v", "v", "s")
-HT_EXIT = ("s", "s")
-G_EXIT = ("s", "v", "s", "s", "v", "s", "v", "s")
+ET_EXIT = "sssv"
+HT_EXIT = "sv"
+G_EXIT = "vssvssss"
+SELF_EXIT = "ssvs"
+PINNED = True
 
 
 def tile_rgcnconv_t_kernel(tc, H, E, RW, SW, out):
@@ -30,6 +32,8 @@ def tile_rgcnconv_t_kernel(tc, H, E, RW, SW, out):
         inp = ctx.enter_context(tc.tile_pool(name="inp", bufs=3))
         work = ctx.enter_context(tc.tile_pool(name="work", bufs=2))
         psum = ctx.enter_context(tc.psum_pool(name="psum", bufs=8))
+        if PINNED:
+            ctx.enter_context(tc.manual_schedule())
 
         st = {}
 
@@ -48,33 +52,38 @@ def tile_rgcnconv_t_kernel(tc, H, E, RW, SW, out):
             for k in range(K):
                 nc.sync.dma_start(out=enat[:, k], in_=E[b, k].rearrange("(c p) j -> p c j", p=P))
 
-        def load_h(b):
+        def load_ha(b):
             ha = inp.tile([P, 4 * F], BF16, name="ha%d" % b, tag="ha")
             st[("ha", b)] = ha
             nc.sync.dma_start(
                 out=ha[:].rearrange("p (u x) -> p u x", u=2),
                 in_=H[b].rearrange("(u p e) m -> p u (e m)", u=2, e=2),
             )
+
+        def load_hb(b):
             hb = inp.tile([P, 4, F], BF16, name="hb%d" % b, tag="hb")
             st[("hb", b)] = hb
             nc.sync.dma_start(out=hb[:], in_=H[b].rearrange("(c p) m -> p c m", p=P))
-
-        load_e(0)
-        load_h(0)
-        rw_raw = const.tile([P, 4, F * K], BF16, name="rw_raw")
-        nc.sync.dma_start(out=rw_raw[:], in_=RW.rearrange("(t p) f k -> p t (f k)", p=P))
-        sw_sb = const.tile([P, 2, 2, F], BF16, name="sw_sb")
-        nc.sync.dma_start(
-            out=sw_sb[:].rearrange("w u e f -> w u (e f)"),
-            in_=SW.rearrange("(u w e) f -> w u (e f)", u=2, e=2),
-        )
-        load_e(1)
-        load_h(1)
 
         ident = const.tile([P, P], F32, name="ident")
         make_identity(nc, ident[:])
         ones = const.tile([P, 32], BF16, name="ones")
         nc.vector.memset(ones[:], 1.0)
+
+        load_hb(0)
+        sw_sb = const.tile([P, 2, 2, F], BF16, name="sw_sb")
+        nc.sync.dma_start(
+            out=sw_sb[:].rearrange("w u e f -> w u (e f)"),
+            in_=SW.rearrange("(u w e) f -> w u (e f)", u=2, e=2),
+        )
+        load_e(0)
+        load_ha(0)
+        load_hb(1)
+        rw_raw = const.tile([P, 4, F * K], BF16, name="rw_raw")
+        nc.sync.dma_start(out=rw_raw[:], in_=RW.rearrange("(t p) f k -> p t (f k)", p=P))
+        load_e(1)
+        load_ha(1)
+        load_hb(2)
 
         w_grp = const.tile([P, K, 4 * F], BF16, name="w_grp", align_bytes=64)
         w_codes = const.tile([P, K, F], U32, name="w_codes", align_bytes=64)
@@ -89,18 +98,28 @@ def tile_rgcnconv_t_kernel(tc, H, E, RW, SW, out):
                     out=w_codes[:, k, :].bitcast(FP8X4), scales=w_scales[:, k, :], in_=w_grp[:, k, :]
                 )
 
-        def quantise_h(b):
+        def regroup_h(b):
             ha = st[("ha", b)]
             hgr = work.tile([P, 4 * F], BF16, name="hgr%d" % b, tag="hgr", align_bytes=64)
+            st[("hgr", b)] = hgr
             nc.vector.tensor_copy(
                 out=hgr[:].rearrange("p (c i t) -> p c t i", i=4, t=4),
                 in_=ha[:].rearrange("p (t c i) -> p c t i", t=4, i=4),
             )
+
+        def quantise_h(b):
             hc = work.tile([P, F], U32, name="hc%d" % b, tag="hc", align_bytes=64)
             hs = work.tile([P, F], U8, name="hs%d" % b, tag="hs", align_bytes=64)
-            nc.vector.quantize_mx(out=hc[:].bitcast(FP8X4), scales=hs[:], in_=hgr[:])
+            nc.vector.quantize_mx(out=hc[:].bitcast(FP8X4), scales=hs[:], in_=st[("hgr", b)][:])
             st[("hc", b)] = hc
             st[("hs", b)] = hs
+
+        def quantise_e(b, k):
+            ec = work.tile([P, N], U32, name="ec%d_%d" % (b, k), tag="ec", bufs=4, align_bytes=64)
+            es = work.tile([P, N], U8, name="es%d_%d" % (b, k), tag="es", bufs=4, align_bytes=64)
+            nc.vector.quantize_mx(out=ec[:].bitcast(FP8X4), scales=es[:], in_=st[("egr", b, k)][:])
+            st[("ec", b, k)] = ec
+            st[("es", b, k)] = es
 
         def et_op(b, k, h, u, cc):
             if u == 0 and cc == 0:
@@ -123,12 +142,6 @@ def tile_rgcnconv_t_kernel(tc, H, E, RW, SW, out):
                     egr[:].bitcast(F32).rearrange("p (i u) -> p i u", u=2)[:, 256 * h : 256 * h + 256, :],
                     tr[:].rearrange("p (u i) -> p i u", u=2),
                 )
-                if h == 1:
-                    ec = work.tile([P, N], U32, name="ec%d_%d" % (b, k), tag="ec", bufs=4, align_bytes=64)
-                    es = work.tile([P, N], U8, name="es%d_%d" % (b, k), tag="es", bufs=4, align_bytes=64)
-                    nc.vector.quantize_mx(out=ec[:].bitcast(FP8X4), scales=es[:], in_=egr[:])
-                    st[("ec", b, k)] = ec
-                    st[("es", b, k)] = es
 
         def ht_op(b, u, c):
             if c == 0:
@@ -167,33 +180,6 @@ def tile_rgcnconv_t_kernel(tc, H, E, RW, SW, out):
                 nc.vector.reciprocal(out=dinv[:], in_=dsum[:])
                 st[("dinv", b)] = dinv
 
-        def side_ops(b):
-            trs = []
-            for k in range(K):
-                for h in range(2):
-                    for u in range(2):
-                        for cc in range(2):
-                            trs.append(lambda k=k, h=h, u=u, cc=cc: et_op(b, k, h, u, cc))
-            for u in range(2):
-                for c in range(4):
-                    trs.append(lambda u=u, c=c: ht_op(b, u, c))
-            ds = []
-            for c in range(4):
-                for k in range(K):
-                    for c2 in range(4):
-                        ds.append(lambda c=c, k=k, c2=c2: d_op(b, c, k, c2))
-            return merge(trs, ds)
-
-        def merge(main, side):
-            res = []
-            done = 0
-            for idx in range(len(main)):
-                res.append(main[idx])
-                want = (idx + 1) * len(side) // len(main)
-                res.extend(side[done:want])
-                done = want
-            return res
-
         def self_op(b, c, q):
             if q == 0:
                 st["sp"] = bank("sp%d_%d" % (b, c))
@@ -209,16 +195,96 @@ def tile_rgcnconv_t_kernel(tc, H, E, RW, SW, out):
                 stop=(q == 3),
             )
             if q == 3:
-                ssb = work.tile([P, F], F32, name="ssb%d_%d" % (b, c), tag="ssb", bufs=6)
-                nc.scalar.copy(out=ssb[:], in_=sp[:])
+                ssb = work.tile([P, F], F32, name="ssb%d_%d" % (b, c), tag="ssb", bufs=8)
+                evac(SELF_EXIT[c], ssb[:], sp[:])
                 st[("ssb", b, c)] = ssb
 
-        def self_ops(b):
+        def e_transposes(b):
+            ops = []
+            for k in range(K):
+                for h in range(2):
+                    for u in range(2):
+                        for cc in range(2):
+                            ops.append(lambda k=k, h=h, u=u, cc=cc: et_op(b, k, h, u, cc))
+            return ops
+
+        def h_transposes(b):
+            ops = []
+            for u in range(2):
+                for c in range(4):
+                    ops.append(lambda u=u, c=c: ht_op(b, u, c))
+            return ops
+
+        def d_ops(b):
             ops = []
             for c in range(4):
+                for k in range(K):
+                    for c2 in range(4):
+                        ops.append(lambda c=c, k=k, c2=c2: d_op(b, c, k, c2))
+            return ops
+
+        def self_ops(b, cs):
+            ops = []
+            for c in cs:
                 for q in range(4):
                     ops.append(lambda c=c, q=q: self_op(b, c, q))
             return ops
+
+        def sigmoid_store(b, c, width):
+            y = st[("y", b)]
+            nc.scalar.activation(out=y[:, c, :], in_=y[:, c, :], func=ACT.Sigmoid)
+            if (c + 1) % width == 0:
+                nc.sync.dma_start(
+                    out=out[b].rearrange("(c p) f -> p c f", p=P)[:, c + 1 - width : c + 1, :],
+                    in_=y[:, c + 1 - width : c + 1, :],
+                )
+
+        def plain_phase(b):
+            mains = []
+            if b >= 0:
+                mains.extend(self_ops(b, (2, 3)))
+            if b + 1 < B:
+                mains.extend(self_ops(b + 1, (0, 1)))
+            trs = []
+            if b + 1 < B:
+                trs.extend(e_transposes(b + 1))
+            if b + 2 < B:
+                trs.extend(h_transposes(b + 2))
+            seq = []
+            done = 0
+            for i in range(len(mains)):
+                seq.append((("mm", i), mains[i]))
+                want = min(len(trs), (i + 1) * 3 // 2)
+                for j in range(done, want):
+                    seq.append((("tr", j), trs[j]))
+                done = want
+            for j in range(done, len(trs)):
+                seq.append((("tr", j), trs[j]))
+            if b + 1 < B:
+                ds = d_ops(b + 1)
+                for j in range(len(ds)):
+                    seq.append((("d", j), ds[j]))
+            labels = [item[0] for item in seq]
+            extras = {}
+
+            def after(label, op):
+                key = label if label in labels else labels[-1]
+                if key not in extras:
+                    extras[key] = []
+                extras[key].append(op)
+
+            if b + 1 < B:
+                after(("mm", 3), lambda: regroup_h(b + 1))
+                after(("mm", 11), lambda: quantise_h(b + 1))
+                after(("tr", 11), lambda: quantise_e(b + 1, 0))
+                after(("tr", 23), lambda: quantise_e(b + 1, 1))
+            if b >= 1:
+                for c in range(4):
+                    after(("mm", 4 * c + 1), lambda c=c: sigmoid_store(b - 1, c, 2))
+            for label, op in seq:
+                op()
+                for extra in extras.get(label, ()):
+                    extra()
 
         def stage1(b):
             hc = st[("hc", b)]
@@ -255,6 +321,7 @@ def tile_rgcnconv_t_kernel(tc, H, E, RW, SW, out):
             xs = st[("xs", b)]
             dinv = st[("dinv", b)]
             y = work.tile([P, 4, F], F32, name="y%d" % b, tag="y")
+            st[("y", b)] = y
             for c in range(4):
                 r = bank("r%d_%d" % (b, c))
                 for k in range(K):
@@ -275,29 +342,21 @@ def tile_rgcnconv_t_kernel(tc, H, E, RW, SW, out):
                     op0=ALU.mult,
                     op1=ALU.add,
                 )
-                nc.scalar.activation(out=y[:, c, :], in_=y[:, c, :], func=ACT.Sigmoid)
-                if c % 2 == 1:
-                    nc.sync.dma_start(
-                        out=out[b].rearrange("(c p) f -> p c f", p=P)[:, c - 1 : c + 1, :],
-                        in_=y[:, c - 1 : c + 1, :],
-                    )
+                if b == B - 1:
+                    sigmoid_store(b, c, 1)
 
-        quantise_h(0)
-        for op in side_ops(0):
+        for op in h_transposes(0):
             op()
+        plain_phase(-1)
         quantise_w()
         stage1(0)
         for b in range(B):
             if b + 2 < B:
                 load_e(b + 2)
-                load_h(b + 2)
-            if b + 1 < B:
-                quantise_h(b + 1)
-                for op in merge(self_ops(b), side_ops(b + 1)):
-                    op()
-            else:
-                for op in self_ops(b):
-                    op()
+                load_ha(b + 2)
+            if b + 3 < B:
+                load_hb(b + 3)
+            plain_phase(b)
             stage2(b)
             if b + 1 < B:
                 stage1(b + 1)

@@ -18,10 +18,10 @@ N = 512
 F = 512
 FLOPS = 2 * B * K * N * N * F + 2 * B * N * K * F * F + 2 * B * N * F * F
 
-ET_EXIT = "sssv"
-HT_EXIT = "sv"
-G_EXIT = "vssvssss"
-SELF_EXIT = "ssvs"
+ET_EXIT = {"all": "sssv", 0: "ssss", 7: "ssss"}
+HT_EXIT = {"all": "sv", 0: "ss"}
+G_EXIT = {"all": "vssvssss", 0: "vssvvsss", 7: "sssvvsss"}
+SELF_EXIT = {"all": "ssvs", 7: "vsvv"}
 PINNED = True
 
 
@@ -46,11 +46,14 @@ def tile_rgcnconv_t_kernel(tc, H, E, RW, SW, out):
             else:
                 nc.scalar.copy(out=dst, in_=src)
 
-        def load_e(b):
-            enat = inp.tile([P, K, 4, N], BF16, name="enat%d" % b, tag="enat")
-            st[("enat", b)] = enat
-            for k in range(K):
-                nc.sync.dma_start(out=enat[:, k], in_=E[b, k].rearrange("(c p) j -> p c j", p=P))
+        def load_e(b, k, pieces):
+            if k == 0:
+                st[("enat", b)] = inp.tile([P, K, 4, N], BF16, name="enat%d" % b, tag="enat")
+            enat = st[("enat", b)]
+            src = E[b, k].rearrange("(c p) j -> p c j", p=P)
+            step = 4 // pieces
+            for c0 in range(0, 4, step):
+                nc.sync.dma_start(out=enat[:, k, c0 : c0 + step], in_=src[:, c0 : c0 + step])
 
         def load_ha(b):
             ha = inp.tile([P, 4 * F], BF16, name="ha%d" % b, tag="ha")
@@ -70,18 +73,20 @@ def tile_rgcnconv_t_kernel(tc, H, E, RW, SW, out):
         ones = const.tile([P, 32], BF16, name="ones")
         nc.vector.memset(ones[:], 1.0)
 
+        load_e(0, 0, 2)
+        load_ha(0)
+        load_e(0, 1, 2)
         load_hb(0)
         sw_sb = const.tile([P, 2, 2, F], BF16, name="sw_sb")
         nc.sync.dma_start(
             out=sw_sb[:].rearrange("w u e f -> w u (e f)"),
             in_=SW.rearrange("(u w e) f -> w u (e f)", u=2, e=2),
         )
-        load_e(0)
-        load_ha(0)
         load_hb(1)
         rw_raw = const.tile([P, 4, F * K], BF16, name="rw_raw")
         nc.sync.dma_start(out=rw_raw[:], in_=RW.rearrange("(t p) f k -> p t (f k)", p=P))
-        load_e(1)
+        load_e(1, 0, 1)
+        load_e(1, 1, 1)
         load_ha(1)
         load_hb(2)
 
@@ -89,10 +94,12 @@ def tile_rgcnconv_t_kernel(tc, H, E, RW, SW, out):
         w_codes = const.tile([P, K, F], U32, name="w_codes", align_bytes=64)
         w_scales = const.tile([P, K, F], U8, name="w_scales", align_bytes=64)
 
-        def quantise_w():
+        def regroup_w():
             src = rw_raw[:].rearrange("p t (f k) -> p k f t", k=K)
             for k in range(K):
                 evac("vs"[k], w_grp[:, k, :].rearrange("p (f t) -> p f t", t=4), src[:, k])
+
+        def quantise_w():
             for k in range(K):
                 nc.vector.quantize_mx(
                     out=w_codes[:, k, :].bitcast(FP8X4), scales=w_scales[:, k, :], in_=w_grp[:, k, :]
@@ -138,7 +145,7 @@ def tile_rgcnconv_t_kernel(tc, H, E, RW, SW, out):
             if u == 1 and cc == 1:
                 egr = st[("egr", b, k)]
                 evac(
-                    ET_EXIT[2 * k + h],
+                    ET_EXIT.get(b, ET_EXIT["all"])[2 * k + h],
                     egr[:].bitcast(F32).rearrange("p (i u) -> p i u", u=2)[:, 256 * h : 256 * h + 256, :],
                     tr[:].rearrange("p (u i) -> p i u", u=2),
                 )
@@ -157,7 +164,7 @@ def tile_rgcnconv_t_kernel(tc, H, E, RW, SW, out):
             )
             if c == 3:
                 ht = st[("ht", b)]
-                evac(HT_EXIT[u], ht[:, u].rearrange("p n e -> p (n e)").bitcast(F32), tr[:])
+                evac(HT_EXIT.get(b, HT_EXIT["all"])[u], ht[:, u].rearrange("p n e -> p (n e)").bitcast(F32), tr[:])
 
         def d_op(b, c, k, c2):
             if c == 0 and k == 0 and c2 == 0:
@@ -196,7 +203,7 @@ def tile_rgcnconv_t_kernel(tc, H, E, RW, SW, out):
             )
             if q == 3:
                 ssb = work.tile([P, F], F32, name="ssb%d_%d" % (b, c), tag="ssb", bufs=8)
-                evac(SELF_EXIT[c], ssb[:], sp[:])
+                evac(SELF_EXIT.get(b, SELF_EXIT["all"])[c], ssb[:], sp[:])
                 st[("ssb", b, c)] = ssb
 
         def e_transposes(b):
@@ -232,17 +239,13 @@ def tile_rgcnconv_t_kernel(tc, H, E, RW, SW, out):
 
         def sigmoid_store(b, c, width):
             y = st[("y", b)]
-            nc.scalar.activation(out=y[:, c, :], in_=y[:, c, :], func=ACT.Sigmoid)
-            if (c + 1) % width == 0:
-                nc.sync.dma_start(
-                    out=out[b].rearrange("(c p) f -> p c f", p=P)[:, c + 1 - width : c + 1, :],
-                    in_=y[:, c + 1 - width : c + 1, :],
-                )
+            nc.scalar.activation(out=y[:, c : c + width, :], in_=y[:, c : c + width, :], func=ACT.Sigmoid)
+            nc.sync.dma_start(
+                out=out[b].rearrange("(c p) f -> p c f", p=P)[:, c : c + width, :], in_=y[:, c : c + width, :]
+            )
 
         def plain_phase(b):
-            mains = []
-            if b >= 0:
-                mains.extend(self_ops(b, (2, 3)))
+            mains = self_ops(b, (2, 3))
             if b + 1 < B:
                 mains.extend(self_ops(b + 1, (0, 1)))
             trs = []
@@ -279,8 +282,8 @@ def tile_rgcnconv_t_kernel(tc, H, E, RW, SW, out):
                 after(("tr", 11), lambda: quantise_e(b + 1, 0))
                 after(("tr", 23), lambda: quantise_e(b + 1, 1))
             if b >= 1:
-                for c in range(4):
-                    after(("mm", 4 * c + 1), lambda c=c: sigmoid_store(b - 1, c, 2))
+                after(("mm", 3), lambda: sigmoid_store(b - 1, 0, 2))
+                after(("mm", 11), lambda: sigmoid_store(b - 1, 2, 2))
             for label, op in seq:
                 op()
                 for extra in extras.get(label, ()):
@@ -310,7 +313,7 @@ def tile_rgcnconv_t_kernel(tc, H, E, RW, SW, out):
                             stop=True,
                         )
                     evac(
-                        G_EXIT[4 * k + ib],
+                        G_EXIT.get(b, G_EXIT["all"])[4 * k + ib],
                         xgr[:, k, :].rearrange("p (i t) -> p i t", t=4)[:, 128 * ib : 128 * ib + 128, :],
                         g[:].rearrange("p (t i) -> p i t", t=4),
                     )
@@ -334,25 +337,50 @@ def tile_rgcnconv_t_kernel(tc, H, E, RW, SW, out):
                         start=(k == 0),
                         stop=(k == K - 1),
                     )
-                nc.vector.scalar_tensor_tensor(
-                    out=y[:, c, :],
-                    in0=r[:],
-                    scalar=dinv[:, c : c + 1],
-                    in1=st[("ssb", b, c)][:],
-                    op0=ALU.mult,
-                    op1=ALU.add,
-                )
-                if b == B - 1:
-                    sigmoid_store(b, c, 1)
+                pieces = 2 if (b == B - 1 and c == 3) else 1
+                width = F // pieces
+                for f0 in range(0, F, width):
+                    nc.vector.scalar_tensor_tensor(
+                        out=y[:, c, f0 : f0 + width],
+                        in0=r[:, f0 : f0 + width],
+                        scalar=dinv[:, c : c + 1],
+                        in1=st[("ssb", b, c)][:, f0 : f0 + width],
+                        op0=ALU.mult,
+                        op1=ALU.add,
+                    )
+                    if b == B - 1:
+                        nc.scalar.activation(
+                            out=y[:, c, f0 : f0 + width], in_=y[:, c, f0 : f0 + width], func=ACT.Sigmoid
+                        )
+                        nc.sync.dma_start(
+                            out=out[b, 128 * c : 128 * c + 128, f0 : f0 + width], in_=y[:, c, f0 : f0 + width]
+                        )
 
+        first = e_transposes(0)
+        for op in first[0:8]:
+            op()
+        regroup_h(0)
+        quantise_h(0)
+        quantise_e(0, 0)
+        for op in first[8:16]:
+            op()
+        quantise_e(0, 1)
+        stage1(0)
+        for op in d_ops(0):
+            op()
         for op in h_transposes(0):
             op()
-        plain_phase(-1)
+        regroup_w()
+        mains = self_ops(0, (0, 1))
+        trs = h_transposes(1)
+        for i in range(8):
+            mains[i]()
+            trs[i]()
         quantise_w()
-        stage1(0)
         for b in range(B):
             if b + 2 < B:
-                load_e(b + 2)
+                load_e(b + 2, 0, 1)
+                load_e(b + 2, 1, 1)
                 load_ha(b + 2)
             if b + 3 < B:
                 load_hb(b + 3)

@@ -55,40 +55,34 @@ def tile_rgcnconv_t_kernel(tc, H, E, RW, SW, out):
             for c0 in range(0, 4, step):
                 nc.sync.dma_start(out=enat[:, k, c0 : c0 + step], in_=src[:, c0 : c0 + step])
 
-        def load_ha(b):
-            ha = inp.tile([P, 4 * F], BF16, name="ha%d" % b, tag="ha")
+        def load_ha(b, pieces=1):
+            ha = inp.tile([P, 4 * F], BF16, name="ha%d" % b, tag="ha", bufs=4)
             st[("ha", b)] = ha
-            nc.sync.dma_start(
-                out=ha[:].rearrange("p (u x) -> p u x", u=2),
-                in_=H[b].rearrange("(u p e) m -> p u (e m)", u=2, e=2),
-            )
-
-        def load_hb(b):
-            hb = inp.tile([P, 4, F], BF16, name="hb%d" % b, tag="hb")
-            st[("hb", b)] = hb
-            nc.sync.dma_start(out=hb[:], in_=H[b].rearrange("(c p) m -> p c m", p=P))
+            dst = ha[:].rearrange("p (u x) -> p u x", u=2)
+            src = H[b].rearrange("(u p e) m -> p u (e m)", u=2, e=2)
+            step = 2 // pieces
+            for u0 in range(0, 2, step):
+                nc.sync.dma_start(out=dst[:, u0 : u0 + step], in_=src[:, u0 : u0 + step])
 
         ident = const.tile([P, P], F32, name="ident")
         make_identity(nc, ident[:])
         ones = const.tile([P, 32], BF16, name="ones")
         nc.vector.memset(ones[:], 1.0)
 
-        load_e(0, 0, 2)
-        load_ha(0)
-        load_e(0, 1, 2)
-        load_hb(0)
+        load_ha(0, 2)
         sw_sb = const.tile([P, 2, 2, F], BF16, name="sw_sb")
-        nc.sync.dma_start(
-            out=sw_sb[:].rearrange("w u e f -> w u (e f)"),
-            in_=SW.rearrange("(u w e) f -> w u (e f)", u=2, e=2),
-        )
-        load_hb(1)
+        sw_dst = sw_sb[:].rearrange("w u e f -> w u (e f)")
+        sw_src = SW.rearrange("(u w e) f -> w u (e f)", u=2, e=2)
+        for u in range(2):
+            nc.sync.dma_start(out=sw_dst[:, u], in_=sw_src[:, u])
         rw_raw = const.tile([P, 4, F * K], BF16, name="rw_raw")
         nc.sync.dma_start(out=rw_raw[:], in_=RW.rearrange("(t p) f k -> p t (f k)", p=P))
+        load_e(0, 0, 2)
+        load_e(0, 1, 2)
+        load_ha(1)
         load_e(1, 0, 1)
         load_e(1, 1, 1)
-        load_ha(1)
-        load_hb(2)
+        load_ha(2)
 
         w_grp = const.tile([P, K, 4 * F], BF16, name="w_grp", align_bytes=64)
         w_codes = const.tile([P, K, F], U32, name="w_codes", align_bytes=64)
@@ -156,15 +150,19 @@ def tile_rgcnconv_t_kernel(tc, H, E, RW, SW, out):
                 if u == 0:
                     st[("ht", b)] = work.tile([P, 2, N, 2], BF16, name="ht%d" % b, tag="ht")
             tr = st["tr"]
-            hb = st[("hb", b)]
+            ha = st[("ha", b)]
             nc.tensor.transpose(
                 tr[:, 128 * c : 128 * c + 128],
-                hb[:, c, :].bitcast(F32)[:, 128 * u : 128 * u + 128],
+                ha[:, 512 * c : 512 * c + 512].bitcast(F32)[:, 128 * u : 128 * u + 128],
                 ident[:],
             )
             if c == 3:
                 ht = st[("ht", b)]
-                evac(HT_EXIT.get(b, HT_EXIT["all"])[u], ht[:, u].rearrange("p n e -> p (n e)").bitcast(F32), tr[:])
+                evac(
+                    HT_EXIT.get(b, HT_EXIT["all"])[u],
+                    ht[:, u].rearrange("p n e -> p (n e)").bitcast(F32).rearrange("p (v q s) -> p v q s", v=2, s=2),
+                    tr[:].rearrange("p (v s q) -> p v q s", v=2, s=2),
+                )
 
         def d_op(b, c, k, c2):
             if c == 0 and k == 0 and c2 == 0:
@@ -245,7 +243,7 @@ def tile_rgcnconv_t_kernel(tc, H, E, RW, SW, out):
             )
 
         def plain_phase(b):
-            mains = self_ops(b, (2, 3))
+            mains = self_ops(b, (2, 3)) if b > 0 else []
             if b + 1 < B:
                 mains.extend(self_ops(b + 1, (0, 1)))
             trs = []
@@ -278,7 +276,7 @@ def tile_rgcnconv_t_kernel(tc, H, E, RW, SW, out):
 
             if b + 1 < B:
                 after(("mm", 3), lambda: regroup_h(b + 1))
-                after(("mm", 11), lambda: quantise_h(b + 1))
+                after(("mm", 11 if b else 7), lambda: quantise_h(b + 1))
                 after(("tr", 11), lambda: quantise_e(b + 1, 0))
                 after(("tr", 23), lambda: quantise_e(b + 1, 1))
             if b >= 1:
@@ -356,34 +354,34 @@ def tile_rgcnconv_t_kernel(tc, H, E, RW, SW, out):
                             out=out[b, 128 * c : 128 * c + 128, f0 : f0 + width], in_=y[:, c, f0 : f0 + width]
                         )
 
-        first = e_transposes(0)
-        for op in first[0:8]:
+        for op in h_transposes(0):
             op()
         regroup_h(0)
         quantise_h(0)
-        quantise_e(0, 0)
-        for op in first[8:16]:
-            op()
-        quantise_e(0, 1)
-        stage1(0)
-        for op in d_ops(0):
-            op()
-        for op in h_transposes(0):
+        for op in self_ops(0, (0, 1)):
             op()
         regroup_w()
-        mains = self_ops(0, (0, 1))
-        trs = h_transposes(1)
-        for i in range(8):
-            mains[i]()
-            trs[i]()
+        for op in self_ops(0, (2, 3)):
+            op()
         quantise_w()
+        trs = e_transposes(0)
+        for op in trs[0:8]:
+            op()
+        quantise_e(0, 0)
+        for op in trs[8:16]:
+            op()
+        quantise_e(0, 1)
+        for op in d_ops(0):
+            op()
+        for op in h_transposes(1):
+            op()
+        stage1(0)
         for b in range(B):
             if b + 2 < B:
                 load_e(b + 2, 0, 1)
                 load_e(b + 2, 1, 1)
-                load_ha(b + 2)
             if b + 3 < B:
-                load_hb(b + 3)
+                load_ha(b + 3)
             plain_phase(b)
             stage2(b)
             if b + 1 < B:

@@ -18,11 +18,15 @@ N = 512
 F = 512
 FLOPS = 2 * B * K * N * N * F + 2 * B * N * K * F * F + 2 * B * N * F * F
 
-ET_EXIT = {"all": "sssv", 0: "ssss", 7: "ssss"}
-HT_EXIT = {"all": "sv", 0: "ss"}
-G_EXIT = {"all": "vssvssss", 0: "vssvvsss", 7: "sssvvsss"}
-SELF_EXIT = {"all": "ssvs", 7: "vsvv"}
+ET_EXIT = {"all": "ssss"}
+HT_EXIT = {"all": "sv"}
+G_EXIT = {"all": "svsvssvs", 0: "vssvvsss"}
+SELF_EXIT = {"all": "sssv", 7: "vsvv"}
 PINNED = True
+QX0 = 1
+QE0 = ("tr", 11)
+QE1 = ("tr", 23)
+QX1 = ("mm", 1)
 
 
 def tile_rgcnconv_t_kernel(tc, H, E, RW, SW, out):
@@ -148,7 +152,7 @@ def tile_rgcnconv_t_kernel(tc, H, E, RW, SW, out):
             if c == 0:
                 st["tr"] = bank("trh%d_%d" % (b, u))
                 if u == 0:
-                    st[("ht", b)] = work.tile([P, 2, N, 2], BF16, name="ht%d" % b, tag="ht")
+                    st[("ht", b)] = work.tile([P, 2, N, 2], BF16, name="ht%d" % b, tag="ht", align_bytes=64)
             tr = st["tr"]
             ha = st[("ha", b)]
             nc.tensor.transpose(
@@ -181,9 +185,12 @@ def tile_rgcnconv_t_kernel(tc, H, E, RW, SW, out):
                 nc.vector.tensor_scalar_add(
                     out=dsum[:], in0=dp[:, 0:128].rearrange("p (c n) -> p c n", n=32)[:, :, 0], scalar1=2.0
                 )
-                dinv = work.tile([P, 4], F32, name="dinv%d" % b, tag="dinv", bufs=3)
-                nc.vector.reciprocal(out=dinv[:], in_=dsum[:])
-                st[("dinv", b)] = dinv
+                st[("dsum", b)] = dsum
+
+        def invert_d(b):
+            dinv = work.tile([P, 4], F32, name="dinv%d" % b, tag="dinv", bufs=3)
+            nc.vector.reciprocal(out=dinv[:], in_=st[("dsum", b)][:])
+            st[("dinv", b)] = dinv
 
         def self_op(b, c, q):
             if q == 0:
@@ -274,11 +281,14 @@ def tile_rgcnconv_t_kernel(tc, H, E, RW, SW, out):
                     extras[key] = []
                 extras[key].append(op)
 
+            if b == B - 1:
+                after(("mm", 1), lambda: quantise_x(b, 1))
             if b + 1 < B:
+                after(QX1, lambda: quantise_x(b, 1))
                 after(("mm", 3), lambda: regroup_h(b + 1))
                 after(("mm", 11 if b else 7), lambda: quantise_h(b + 1))
-                after(("tr", 11), lambda: quantise_e(b + 1, 0))
-                after(("tr", 23), lambda: quantise_e(b + 1, 1))
+                after(QE0, lambda: quantise_e(b + 1, 0))
+                after(QE1, lambda: quantise_e(b + 1, 1))
             if b >= 1:
                 after(("mm", 3), lambda: sigmoid_store(b - 1, 0, 2))
                 after(("mm", 11), lambda: sigmoid_store(b - 1, 2, 2))
@@ -293,6 +303,7 @@ def tile_rgcnconv_t_kernel(tc, H, E, RW, SW, out):
             xgr = work.tile([P, K, 4 * N], BF16, name="xgr%d" % b, tag="xgr", align_bytes=64)
             xc = work.tile([P, K, N], U32, name="xc%d" % b, tag="xc", align_bytes=64)
             xs = work.tile([P, K, N], U8, name="xs%d" % b, tag="xs", align_bytes=64)
+            st[("xgr", b)] = xgr
             st[("xc", b)] = xc
             st[("xs", b)] = xs
             for k in range(K):
@@ -315,7 +326,13 @@ def tile_rgcnconv_t_kernel(tc, H, E, RW, SW, out):
                         xgr[:, k, :].rearrange("p (i t) -> p i t", t=4)[:, 128 * ib : 128 * ib + 128, :],
                         g[:].rearrange("p (t i) -> p i t", t=4),
                     )
-                nc.vector.quantize_mx(out=xc[:, k, :].bitcast(FP8X4), scales=xs[:, k, :], in_=xgr[:, k, :])
+                    if k == 1 and ib == QX0:
+                        quantise_x(b, 0)
+
+        def quantise_x(b, k):
+            nc.vector.quantize_mx(
+                out=st[("xc", b)][:, k, :].bitcast(FP8X4), scales=st[("xs", b)][:, k, :], in_=st[("xgr", b)][:, k, :]
+            )
 
         def stage2(b):
             xc = st[("xc", b)]
@@ -335,6 +352,8 @@ def tile_rgcnconv_t_kernel(tc, H, E, RW, SW, out):
                         start=(k == 0),
                         stop=(k == K - 1),
                     )
+                if c == 1 and b + 1 < B:
+                    invert_d(b + 1)
                 pieces = 2 if (b == B - 1 and c == 3) else 1
                 width = F // pieces
                 for f0 in range(0, F, width):
@@ -375,6 +394,7 @@ def tile_rgcnconv_t_kernel(tc, H, E, RW, SW, out):
             op()
         for op in h_transposes(1):
             op()
+        invert_d(0)
         stage1(0)
         for b in range(B):
             if b + 2 < B:

@@ -18,12 +18,13 @@ N = 512
 F = 512
 FLOPS = 2 * B * K * N * N * F + 2 * B * N * K * F * F + 2 * B * N * F * F
 
-ET_EXIT = {"all": "ssss"}
-HT_EXIT = {"all": "sv"}
+ET_EXIT = {"all": "svsv"}
+HT_EXIT = {"all": "ss"}
 G_EXIT = {"all": "svsvssvs", 0: "vssvvsss"}
-SELF_EXIT = {"all": "sssv", 7: "vsvv"}
+SELF_EXIT = {"all": "ssss", 7: "vsvv"}
 PINNED = True
 QX0 = 1
+QH = ("d", 1)
 QE0 = ("tr", 11)
 QE1 = ("tr", 23)
 QX1 = ("mm", 1)
@@ -105,12 +106,23 @@ def tile_rgcnconv_t_kernel(tc, H, E, RW, SW, out):
 
         def regroup_h(b):
             ha = st[("ha", b)]
-            hgr = work.tile([P, 4 * F], BF16, name="hgr%d" % b, tag="hgr", align_bytes=64)
+            hgr = work.tile([P, 4 * F], BF16, name="hgr%d" % b, tag="hgr", bufs=1, align_bytes=64)
             st[("hgr", b)] = hgr
-            nc.vector.tensor_copy(
-                out=hgr[:].rearrange("p (c i t) -> p c t i", i=4, t=4),
-                in_=ha[:].rearrange("p (t c i) -> p c t i", t=4, i=4),
-            )
+            if b == 0:
+                nc.vector.tensor_copy(
+                    out=hgr[:].rearrange("p (c i t) -> p c t i", i=4, t=4),
+                    in_=ha[:].rearrange("p (t c i) -> p c t i", t=4, i=4),
+                )
+                return
+            for q in range(4):
+                nc.gpsimd.tensor_scalar(
+                    out=hgr[:, 512 * q : 512 * q + 512].rearrange("p (m t) -> p m t", t=4),
+                    in0=ha[:].rearrange("p (t m) -> p m t", t=4)[:, 128 * q : 128 * q + 128],
+                    scalar1=1.0,
+                    scalar2=0.0,
+                    op0=ALU.mult,
+                    op1=ALU.add,
+                )
 
         def quantise_h(b):
             hc = work.tile([P, F], U32, name="hc%d" % b, tag="hc", align_bytes=64)
@@ -286,9 +298,9 @@ def tile_rgcnconv_t_kernel(tc, H, E, RW, SW, out):
             if b + 1 < B:
                 after(QX1, lambda: quantise_x(b, 1))
                 after(("mm", 3), lambda: regroup_h(b + 1))
-                after(("mm", 11 if b else 7), lambda: quantise_h(b + 1))
                 after(QE0, lambda: quantise_e(b + 1, 0))
                 after(QE1, lambda: quantise_e(b + 1, 1))
+                after(QH, lambda: quantise_h(b + 1))
             if b >= 1:
                 after(("mm", 3), lambda: sigmoid_store(b - 1, 0, 2))
                 after(("mm", 11), lambda: sigmoid_store(b - 1, 2, 2))

@@ -18,12 +18,13 @@ N = 512
 F = 512
 FLOPS = 2 * B * K * N * N * F + 2 * B * N * K * F * F + 2 * B * N * F * F
 
-ET_EXIT = {"all": "svsv"}
-HT_EXIT = {"all": "ss"}
+ET_EXIT = {"all": "svss"}
+HT_EXIT = {"all": "vs"}
 G_EXIT = {"all": "svsvssvs", 0: "vssvvsss"}
-SELF_EXIT = {"all": "ssss", 7: "vsvv"}
+SELF_EXIT = {"all": "ssvs", 7: "vsvv"}
 PINNED = True
 QX0 = 1
+WARM = 5
 QH = ("d", 1)
 QE0 = ("tr", 11)
 QE1 = ("tr", 23)
@@ -75,6 +76,13 @@ def tile_rgcnconv_t_kernel(tc, H, E, RW, SW, out):
         nc.vector.memset(ones[:], 1.0)
 
         load_ha(0, 2)
+        warm_act = const.tile([P, 32], F32, name="warm_act")
+        nc.scalar.activation(out=warm_act[:], in_=ones[:], func=ACT.Sigmoid)
+        warm = const.tile([P, F], BF16, name="warm")
+        nc.gpsimd.memset(warm[:], 0.0)
+        wb = bank("warm")
+        for i in range(WARM):
+            nc.tensor.matmul(wb[:], lhsT=warm[:, 0:128], rhs=warm[:], start=True, stop=True)
         sw_sb = const.tile([P, 2, 2, F], BF16, name="sw_sb")
         sw_dst = sw_sb[:].rearrange("w u e f -> w u (e f)")
         sw_src = SW.rearrange("(u w e) f -> w u (e f)", u=2, e=2)
@@ -301,9 +309,6 @@ def tile_rgcnconv_t_kernel(tc, H, E, RW, SW, out):
                 after(QE0, lambda: quantise_e(b + 1, 0))
                 after(QE1, lambda: quantise_e(b + 1, 1))
                 after(QH, lambda: quantise_h(b + 1))
-            if b >= 1:
-                after(("mm", 3), lambda: sigmoid_store(b - 1, 0, 2))
-                after(("mm", 11), lambda: sigmoid_store(b - 1, 2, 2))
             for label, op in seq:
                 op()
                 for extra in extras.get(label, ()):
@@ -350,7 +355,10 @@ def tile_rgcnconv_t_kernel(tc, H, E, RW, SW, out):
             xc = st[("xc", b)]
             xs = st[("xs", b)]
             dinv = st[("dinv", b)]
-            y = work.tile([P, 4, F], F32, name="y%d" % b, tag="y")
+            if b >= 1:
+                sigmoid_store(b - 1, 0, 2)
+                sigmoid_store(b - 1, 2, 2)
+            y = work.tile([P, 4, F], F32, name="y%d" % b, tag="y", bufs=3)
             st[("y", b)] = y
             for c in range(4):
                 r = bank("r%d_%d" % (b, c))

@@ -18,13 +18,20 @@ N = 512
 F = 512
 FLOPS = 2 * B * K * N * N * F + 2 * B * N * K * F * F + 2 * B * N * F * F
 
-ET_EXIT = {"all": "svss"}
-HT_EXIT = {"all": "vs"}
-G_EXIT = {"all": "svsvssvs", 0: "vssvvsss"}
-SELF_EXIT = {"all": "ssvs", 7: "vsvv"}
+ET_EXIT = {"all": "ssss"}
+HT_EXIT = {"all": "ss"}
+G_EXIT = {"all": "svsvsvsv"}
+SELF_EXIT = {"all": "sssv", 7: "sssv"}
 PINNED = True
 QX0 = 1
-WARM = 5
+RG = ("mm", 0)
+LASTC = (1, 2, 3)
+SG = ("mm", 5)
+TAIL = {3: (256, 128, 128)}
+RWV = ""
+HS = 4
+QW = ("mm", 7)
+WARM = 4
 QH = ("d", 1)
 QE0 = ("tr", 11)
 QE1 = ("tr", 23)
@@ -88,11 +95,11 @@ def tile_rgcnconv_t_kernel(tc, H, E, RW, SW, out):
         sw_src = SW.rearrange("(u w e) f -> w u (e f)", u=2, e=2)
         for u in range(2):
             nc.sync.dma_start(out=sw_dst[:, u], in_=sw_src[:, u])
-        rw_raw = const.tile([P, 4, F * K], BF16, name="rw_raw")
-        nc.sync.dma_start(out=rw_raw[:], in_=RW.rearrange("(t p) f k -> p t (f k)", p=P))
         load_e(0, 0, 2)
         load_e(0, 1, 2)
         load_ha(1)
+        rw_raw = const.tile([P, 4, F * K], BF16, name="rw_raw")
+        nc.sync.dma_start(out=rw_raw[:], in_=RW.rearrange("(t p) f k -> p t (f k)", p=P))
         load_e(1, 0, 1)
         load_e(1, 1, 1)
         load_ha(2)
@@ -104,7 +111,17 @@ def tile_rgcnconv_t_kernel(tc, H, E, RW, SW, out):
         def regroup_w():
             src = rw_raw[:].rearrange("p t (f k) -> p k f t", k=K)
             for k in range(K):
-                evac("vs"[k], w_grp[:, k, :].rearrange("p (f t) -> p f t", t=4), src[:, k])
+                if k == 0 and RWV:
+                    evac(RWV, w_grp[:, k, :].rearrange("p (f t) -> p f t", t=4), src[:, k])
+                else:
+                    nc.gpsimd.tensor_scalar(
+                        out=w_grp[:, k, :].rearrange("p (f t) -> p f t", t=4),
+                        in0=src[:, k],
+                        scalar1=1.0,
+                        scalar2=0.0,
+                        op0=ALU.mult,
+                        op1=ALU.add,
+                    )
 
         def quantise_w():
             for k in range(K):
@@ -114,23 +131,12 @@ def tile_rgcnconv_t_kernel(tc, H, E, RW, SW, out):
 
         def regroup_h(b):
             ha = st[("ha", b)]
-            hgr = work.tile([P, 4 * F], BF16, name="hgr%d" % b, tag="hgr", bufs=1, align_bytes=64)
+            hgr = work.tile([P, 4 * F], BF16, name="hgr%d" % b, tag="hgr", bufs=2, align_bytes=64)
             st[("hgr", b)] = hgr
-            if b == 0:
-                nc.vector.tensor_copy(
-                    out=hgr[:].rearrange("p (c i t) -> p c t i", i=4, t=4),
-                    in_=ha[:].rearrange("p (t c i) -> p c t i", t=4, i=4),
-                )
-                return
-            for q in range(4):
-                nc.gpsimd.tensor_scalar(
-                    out=hgr[:, 512 * q : 512 * q + 512].rearrange("p (m t) -> p m t", t=4),
-                    in0=ha[:].rearrange("p (t m) -> p m t", t=4)[:, 128 * q : 128 * q + 128],
-                    scalar1=1.0,
-                    scalar2=0.0,
-                    op0=ALU.mult,
-                    op1=ALU.add,
-                )
+            nc.vector.tensor_copy(
+                out=hgr[:].rearrange("p (c i t) -> p c t i", i=4, t=4),
+                in_=ha[:].rearrange("p (t c i) -> p c t i", t=4, i=4),
+            )
 
         def quantise_h(b):
             hc = work.tile([P, F], U32, name="hc%d" % b, tag="hc", align_bytes=64)
@@ -270,9 +276,9 @@ def tile_rgcnconv_t_kernel(tc, H, E, RW, SW, out):
             )
 
         def plain_phase(b):
-            mains = self_ops(b, (2, 3)) if b > 0 else []
+            mains = self_ops(b, (2, 3) if b < B - 1 else LASTC) if b > 0 else []
             if b + 1 < B:
-                mains.extend(self_ops(b + 1, (0, 1)))
+                mains.extend(self_ops(b + 1, (0, 1) if b + 1 < B - 1 else [c for c in range(4) if c not in LASTC]))
             trs = []
             if b + 1 < B:
                 trs.extend(e_transposes(b + 1))
@@ -301,11 +307,15 @@ def tile_rgcnconv_t_kernel(tc, H, E, RW, SW, out):
                     extras[key] = []
                 extras[key].append(op)
 
+            if b == 0:
+                after(QW, lambda: quantise_w())
             if b == B - 1:
                 after(("mm", 1), lambda: quantise_x(b, 1))
+                after(SG, lambda: sigmoid_store(b - 1, 0, 2))
+                after(SG, lambda: sigmoid_store(b - 1, 2, 2))
             if b + 1 < B:
                 after(QX1, lambda: quantise_x(b, 1))
-                after(("mm", 3), lambda: regroup_h(b + 1))
+                after(RG, lambda: regroup_h(b + 1))
                 after(QE0, lambda: quantise_e(b + 1, 0))
                 after(QE1, lambda: quantise_e(b + 1, 1))
                 after(QH, lambda: quantise_h(b + 1))
@@ -355,65 +365,60 @@ def tile_rgcnconv_t_kernel(tc, H, E, RW, SW, out):
             xc = st[("xc", b)]
             xs = st[("xs", b)]
             dinv = st[("dinv", b)]
-            if b >= 1:
+            if 1 <= b < B - 1:
                 sigmoid_store(b - 1, 0, 2)
                 sigmoid_store(b - 1, 2, 2)
-            y = work.tile([P, 4, F], F32, name="y%d" % b, tag="y", bufs=3)
+            y = work.tile([P, 4, F], F32, name="y%d" % b, tag="y", bufs=B)
             st[("y", b)] = y
             for c in range(4):
-                r = bank("r%d_%d" % (b, c))
-                for k in range(K):
-                    nc.tensor.matmul_mx(
-                        out=r[:],
-                        lhsT=xc[:, k, 128 * c : 128 * c + 128].bitcast(FP8X4),
-                        lhsT_scale=xs[:, k, 128 * c : 128 * c + 128],
-                        rhs=w_codes[:, k, :].bitcast(FP8X4),
-                        rhs_scale=w_scales[:, k, :],
-                        start=(k == 0),
-                        stop=(k == K - 1),
-                    )
                 if c == 1 and b + 1 < B:
                     invert_d(b + 1)
-                pieces = 2 if (b == B - 1 and c == 3) else 1
-                width = F // pieces
-                for f0 in range(0, F, width):
+                widths = TAIL.get(c, (F,)) if b == B - 1 else (F,)
+                f0 = 0
+                for width in widths:
+                    fs = slice(f0, f0 + width)
+                    r = bank("r%d_%d_%d" % (b, c, f0))
+                    for k in range(K):
+                        nc.tensor.matmul_mx(
+                            out=r[:, 0:width],
+                            lhsT=xc[:, k, 128 * c : 128 * c + 128].bitcast(FP8X4),
+                            lhsT_scale=xs[:, k, 128 * c : 128 * c + 128],
+                            rhs=w_codes[:, k, fs].bitcast(FP8X4),
+                            rhs_scale=w_scales[:, k, fs],
+                            start=(k == 0),
+                            stop=(k == K - 1),
+                        )
                     nc.vector.scalar_tensor_tensor(
-                        out=y[:, c, f0 : f0 + width],
-                        in0=r[:, f0 : f0 + width],
+                        out=y[:, c, fs],
+                        in0=r[:, 0:width],
                         scalar=dinv[:, c : c + 1],
-                        in1=st[("ssb", b, c)][:, f0 : f0 + width],
+                        in1=st[("ssb", b, c)][:, fs],
                         op0=ALU.mult,
                         op1=ALU.add,
                     )
                     if b == B - 1:
-                        nc.scalar.activation(
-                            out=y[:, c, f0 : f0 + width], in_=y[:, c, f0 : f0 + width], func=ACT.Sigmoid
-                        )
-                        nc.sync.dma_start(
-                            out=out[b, 128 * c : 128 * c + 128, f0 : f0 + width], in_=y[:, c, f0 : f0 + width]
-                        )
+                        nc.scalar.activation(out=y[:, c, fs], in_=y[:, c, fs], func=ACT.Sigmoid)
+                        nc.sync.dma_start(out=out[b, 128 * c : 128 * c + 128, fs], in_=y[:, c, fs])
+                    f0 += width
 
         for op in h_transposes(0):
             op()
         regroup_h(0)
         quantise_h(0)
-        for op in self_ops(0, (0, 1)):
-            op()
         regroup_w()
-        for op in self_ops(0, (2, 3)):
-            op()
-        quantise_w()
+        mains = self_ops(0, (0, 1, 2, 3))
         trs = e_transposes(0)
-        for op in trs[0:8]:
-            op()
-        quantise_e(0, 0)
-        for op in trs[8:16]:
-            op()
-        quantise_e(0, 1)
+        for i in range(16):
+            mains[i]()
+            for j in range(max(0, min(16, (i - HS) * 3 // 2)), max(0, min(16, (i + 1 - HS) * 3 // 2))):
+                trs[j]()
+                if j == 11:
+                    quantise_e(0, 0)
         for op in d_ops(0):
             op()
         for op in h_transposes(1):
             op()
+        quantise_e(0, 1)
         invert_d(0)
         stage1(0)
         for b in range(B):

@@ -19,11 +19,12 @@ F = 512
 FLOPS = 2 * B * K * N * N * F + 2 * B * N * K * F * F + 2 * B * N * F * F
 
 ET_EXIT = {"all": "ssss"}
-HT_EXIT = {"all": "ss"}
+HT_EXIT = {"all": "ss", 0: "vs"}
 G_EXIT = {"all": "svsvsvsv"}
 SELF_EXIT = {"all": "sssv", 7: "sssv"}
 PINNED = True
 QX0 = 1
+HP = 4
 RG = ("mm", 0)
 LASTC = (1, 2, 3)
 SG = ("mm", 5)
@@ -68,33 +69,31 @@ def tile_rgcnconv_t_kernel(tc, H, E, RW, SW, out):
             for c0 in range(0, 4, step):
                 nc.sync.dma_start(out=enat[:, k, c0 : c0 + step], in_=src[:, c0 : c0 + step])
 
-        def load_ha(b, pieces=1):
-            ha = inp.tile([P, 4 * F], BF16, name="ha%d" % b, tag="ha", bufs=4)
-            st[("ha", b)] = ha
-            dst = ha[:].rearrange("p (u x) -> p u x", u=2)
+        def load_ha(b, halves=(0, 1)):
+            if 0 in halves:
+                st[("ha", b)] = inp.tile([P, 4 * F], BF16, name="ha%d" % b, tag="ha", bufs=4)
+            dst = st[("ha", b)][:].rearrange("p (u x) -> p u x", u=2)
             src = H[b].rearrange("(u p e) m -> p u (e m)", u=2, e=2)
-            step = 2 // pieces
-            for u0 in range(0, 2, step):
-                nc.sync.dma_start(out=dst[:, u0 : u0 + step], in_=src[:, u0 : u0 + step])
+            us = slice(halves[0], halves[-1] + 1)
+            nc.sync.dma_start(out=dst[:, us], in_=src[:, us])
 
-        ident = const.tile([P, P], F32, name="ident")
-        make_identity(nc, ident[:])
-        ones = const.tile([P, 32], BF16, name="ones")
-        nc.vector.memset(ones[:], 1.0)
-
-        load_ha(0, 2)
-        warm_act = const.tile([P, 32], F32, name="warm_act")
-        nc.scalar.activation(out=warm_act[:], in_=ones[:], func=ACT.Sigmoid)
         warm = const.tile([P, F], BF16, name="warm")
-        nc.gpsimd.memset(warm[:], 0.0)
+        nc.vector.memset(warm[:], 0.0)
         wb = bank("warm")
         for i in range(WARM):
             nc.tensor.matmul(wb[:], lhsT=warm[:, 0:128], rhs=warm[:], start=True, stop=True)
+        ident = const.tile([P, P], F32, name="ident")
+        make_identity(nc, ident[:])
+        ones = const.tile([P, 16], BF16, name="ones")
+        nc.vector.memset(ones[:], 1.0)
         sw_sb = const.tile([P, 2, 2, F], BF16, name="sw_sb")
         sw_dst = sw_sb[:].rearrange("w u e f -> w u (e f)")
         sw_src = SW.rearrange("(u w e) f -> w u (e f)", u=2, e=2)
         for u in range(2):
+            load_ha(0, (u,))
             nc.sync.dma_start(out=sw_dst[:, u], in_=sw_src[:, u])
+        warm_act = const.tile([P, 16], F32, name="warm_act")
+        nc.scalar.activation(out=warm_act[:], in_=ones[:], func=ACT.Sigmoid)
         load_e(0, 0, 2)
         load_e(0, 1, 2)
         load_ha(1)
@@ -174,24 +173,27 @@ def tile_rgcnconv_t_kernel(tc, H, E, RW, SW, out):
                     tr[:].rearrange("p (u i) -> p i u", u=2),
                 )
 
-        def ht_op(b, u, c):
-            if c == 0:
-                st["tr"] = bank("trh%d_%d" % (b, u))
-                if u == 0:
+        def ht_op(b, v, i):
+            u = i // 2
+            s = i % 2
+            if i == 0:
+                st["tr"] = bank("trh%d_%d" % (b, v))
+                if v == 0:
                     st[("ht", b)] = work.tile([P, 2, N, 2], BF16, name="ht%d" % b, tag="ht", align_bytes=64)
             tr = st["tr"]
             ha = st[("ha", b)]
+            c = 2 * v + s
             nc.tensor.transpose(
-                tr[:, 128 * c : 128 * c + 128],
+                tr[:, 128 * i : 128 * i + 128],
                 ha[:, 512 * c : 512 * c + 512].bitcast(F32)[:, 128 * u : 128 * u + 128],
                 ident[:],
             )
-            if c == 3:
-                ht = st[("ht", b)]
+            if i == 3:
+                words = st[("ht", b)][:].rearrange("p u n e -> p (u n e)").bitcast(F32)
                 evac(
-                    HT_EXIT.get(b, HT_EXIT["all"])[u],
-                    ht[:, u].rearrange("p n e -> p (n e)").bitcast(F32).rearrange("p (v q s) -> p v q s", v=2, s=2),
-                    tr[:].rearrange("p (v s q) -> p v q s", v=2, s=2),
+                    HT_EXIT.get(b, HT_EXIT["all"])[v],
+                    words.rearrange("p (u v q s) -> p v u q s", u=2, v=2, s=2)[:, v],
+                    tr[:].rearrange("p (u s q) -> p u q s", u=2, s=2),
                 )
 
         def d_op(b, c, k, c2):
@@ -200,7 +202,7 @@ def tile_rgcnconv_t_kernel(tc, H, E, RW, SW, out):
             dp = st["dp"]
             enat = st[("enat", b)]
             nc.tensor.matmul(
-                dp[:, 32 * c : 32 * c + 32],
+                dp[:, 16 * c : 16 * c + 16],
                 lhsT=enat[:, k, c2, 128 * c : 128 * c + 128],
                 rhs=ones[:],
                 start=(k == 0 and c2 == 0),
@@ -208,8 +210,8 @@ def tile_rgcnconv_t_kernel(tc, H, E, RW, SW, out):
             )
             if c == 3 and k == K - 1 and c2 == 3:
                 dsum = work.tile([P, 4], F32, name="dsum%d" % b, tag="dsum")
-                nc.vector.tensor_scalar_add(
-                    out=dsum[:], in0=dp[:, 0:128].rearrange("p (c n) -> p c n", n=32)[:, :, 0], scalar1=2.0
+                nc.scalar.activation(
+                    out=dsum[:], in_=dp[:, 0:64].rearrange("p (c n) -> p c n", n=16)[:, :, 0], func=ACT.Copy, bias=2.0
                 )
                 st[("dsum", b)] = dsum
 
@@ -220,8 +222,8 @@ def tile_rgcnconv_t_kernel(tc, H, E, RW, SW, out):
 
         def self_op(b, c, q):
             if q == 0:
-                st["sp"] = bank("sp%d_%d" % (b, c))
-            sp = st["sp"]
+                st[("sp", b, c)] = bank("sp%d_%d" % (b, c))
+            sp = st[("sp", b, c)]
             ht = st[("ht", b)]
             u = q // 2
             e = q % 2
@@ -248,9 +250,9 @@ def tile_rgcnconv_t_kernel(tc, H, E, RW, SW, out):
 
         def h_transposes(b):
             ops = []
-            for u in range(2):
-                for c in range(4):
-                    ops.append(lambda u=u, c=c: ht_op(b, u, c))
+            for v in range(2):
+                for i in range(4):
+                    ops.append(lambda v=v, i=i: ht_op(b, v, i))
             return ops
 
         def d_ops(b):
@@ -401,14 +403,20 @@ def tile_rgcnconv_t_kernel(tc, H, E, RW, SW, out):
                         nc.sync.dma_start(out=out[b, 128 * c : 128 * c + 128, fs], in_=y[:, c, fs])
                     f0 += width
 
-        for op in h_transposes(0):
+        trs = h_transposes(0)
+        for op in trs[0:4]:
+            op()
+        mains = self_ops(0, (0, 1, 2, 3))
+        mains = mains[0:2] + mains[4:6] + mains[2:4] + mains[6:]
+        for i in range(HP):
+            mains[i]()
+        for op in trs[4:8]:
             op()
         regroup_h(0)
         quantise_h(0)
         regroup_w()
-        mains = self_ops(0, (0, 1, 2, 3))
         trs = e_transposes(0)
-        for i in range(16):
+        for i in range(HP, 16):
             mains[i]()
             for j in range(max(0, min(16, (i - HS) * 3 // 2)), max(0, min(16, (i + 1 - HS) * 3 // 2))):
                 trs[j]()

from contextlib import ExitStack

import concourse.mybir as mybir
from concourse.masks import make_identity

F32 = mybir.dt.float32
BF16 = mybir.dt.bfloat16
U32 = mybir.dt.uint32
U8 = mybir.dt.uint8
FP8X4 = mybir.dt.float8_e4m3fn_x4
ACT = mybir.ActivationFunctionType
ALU = mybir.AluOpType

P = 128
B = 8
K = 2
N = 512
F = 512
FLOPS = 2 * B * K * N * N * F + 2 * B * N * K * F * F + 2 * B * N * F * F

ET_EXIT = {"all": "ssss"}
HT_EXIT = {"all": "ss", 0: "vs"}
G_EXIT = {"all": "svsvsvsv"}
SELF_EXIT = {"all": "sssv", 7: "sssv"}
PINNED = True
QX0 = 1
HP = 4
RG = ("mm", 0)
LASTC = (1, 2, 3)
SG = ("mm", 5)
TAIL = {3: (256, 128, 128)}
RWV = ""
HS = 4
QW = ("mm", 7)
WARM = 4
QH = ("d", 1)
QE0 = ("tr", 11)
QE1 = ("tr", 23)
QX1 = ("mm", 1)


def tile_rgcnconv_t_kernel(tc, H, E, RW, SW, out):
    nc = tc.nc
    with ExitStack() as ctx:
        const = ctx.enter_context(tc.tile_pool(name="const", bufs=1))
        inp = ctx.enter_context(tc.tile_pool(name="inp", bufs=3))
        work = ctx.enter_context(tc.tile_pool(name="work", bufs=2))
        psum = ctx.enter_context(tc.psum_pool(name="psum", bufs=8))
        if PINNED:
            ctx.enter_context(tc.manual_schedule())

        st = {}

        def bank(name):
            return psum.tile([P, 512], F32, name=name, tag="bank")

        def evac(eng, dst, src):
            if eng == "v":
                nc.vector.tensor_copy(out=dst, in_=src)
            else:
                nc.scalar.copy(out=dst, in_=src)

        def load_e(b, k, pieces):
            if k == 0:
                st[("enat", b)] = inp.tile([P, K, 4, N], BF16, name="enat%d" % b, tag="enat")
            enat = st[("enat", b)]
            src = E[b, k].rearrange("(c p) j -> p c j", p=P)
            step = 4 // pieces
            for c0 in range(0, 4, step):
                nc.sync.dma_start(out=enat[:, k, c0 : c0 + step], in_=src[:, c0 : c0 + step])

        def load_ha(b, halves=(0, 1)):
            if 0 in halves:
                st[("ha", b)] = inp.tile([P, 4 * F], BF16, name="ha%d" % b, tag="ha", bufs=4)
            dst = st[("ha", b)][:].rearrange("p (u x) -> p u x", u=2)
            src = H[b].rearrange("(u p e) m -> p u (e m)", u=2, e=2)
            us = slice(halves[0], halves[-1] + 1)
            nc.sync.dma_start(out=dst[:, us], in_=src[:, us])

        warm = const.tile([P, F], BF16, name="warm")
        nc.vector.memset(warm[:], 0.0)
        wb = bank("warm")
        for i in range(WARM):
            nc.tensor.matmul(wb[:], lhsT=warm[:, 0:128], rhs=warm[:], start=True, stop=True)
        ident = const.tile([P, P], F32, name="ident")
        make_identity(nc, ident[:])
        ones = const.tile([P, 16], BF16, name="ones")
        nc.vector.memset(ones[:], 1.0)
        sw_sb = const.tile([P, 2, 2, F], BF16, name="sw_sb")
        sw_dst = sw_sb[:].rearrange("w u e f -> w u (e f)")
        sw_src = SW.rearrange("(u w e) f -> w u (e f)", u=2, e=2)
        for u in range(2):
            load_ha(0, (u,))
            nc.sync.dma_start(out=sw_dst[:, u], in_=sw_src[:, u])
        warm_act = const.tile([P, 16], F32, name="warm_act")
        nc.scalar.activation(out=warm_act[:], in_=ones[:], func=ACT.Sigmoid)
        load_e(0, 0, 2)
        load_e(0, 1, 2)
        load_ha(1)
        rw_raw = const.tile([P, 4, F * K], BF16, name="rw_raw")
        nc.sync.dma_start(out=rw_raw[:], in_=RW.rearrange("(t p) f k -> p t (f k)", p=P))
        load_e(1, 0, 1)
        load_e(1, 1, 1)
        load_ha(2)

        w_grp = const.tile([P, K, 4 * F], BF16, name="w_grp", align_bytes=64)
        w_codes = const.tile([P, K, F], U32, name="w_codes", align_bytes=64)
        w_scales = const.tile([P, K, F], U8, name="w_scales", align_bytes=64)

        def regroup_w():
            src = rw_raw[:].rearrange("p t (f k) -> p k f t", k=K)
            for k in range(K):
                if k == 0 and RWV:
                    evac(RWV, w_grp[:, k, :].rearrange("p (f t) -> p f t", t=4), src[:, k])
                else:
                    nc.gpsimd.tensor_scalar(
                        out=w_grp[:, k, :].rearrange("p (f t) -> p f t", t=4),
                        in0=src[:, k],
                        scalar1=1.0,
                        scalar2=0.0,
                        op0=ALU.mult,
                        op1=ALU.add,
                    )

        def quantise_w():
            for k in range(K):
                nc.vector.quantize_mx(
                    out=w_codes[:, k, :].bitcast(FP8X4), scales=w_scales[:, k, :], in_=w_grp[:, k, :]
                )

        def regroup_h(b):
            ha = st[("ha", b)]
            hgr = work.tile([P, 4 * F], BF16, name="hgr%d" % b, tag="hgr", bufs=2, align_bytes=64)
            st[("hgr", b)] = hgr
            nc.vector.tensor_copy(
                out=hgr[:].rearrange("p (c i t) -> p c t i", i=4, t=4),
                in_=ha[:].rearrange("p (t c i) -> p c t i", t=4, i=4),
            )

        def quantise_h(b):
            hc = work.tile([P, F], U32, name="hc%d" % b, tag="hc", align_bytes=64)
            hs = work.tile([P, F], U8, name="hs%d" % b, tag="hs", align_bytes=64)
            nc.vector.quantize_mx(out=hc[:].bitcast(FP8X4), scales=hs[:], in_=st[("hgr", b)][:])
            st[("hc", b)] = hc
            st[("hs", b)] = hs

        def quantise_e(b, k):
            ec = work.tile([P, N], U32, name="ec%d_%d" % (b, k), tag="ec", bufs=4, align_bytes=64)
            es = work.tile([P, N], U8, name="es%d_%d" % (b, k), tag="es", bufs=4, align_bytes=64)
            nc.vector.quantize_mx(out=ec[:].bitcast(FP8X4), scales=es[:], in_=st[("egr", b, k)][:])
            st[("ec", b, k)] = ec
            st[("es", b, k)] = es

        def et_op(b, k, h, u, cc):
            if u == 0 and cc == 0:
                st["tr"] = bank("tre%d_%d_%d" % (b, k, h))
                if h == 0:
                    st[("egr", b, k)] = work.tile(
                        [P, 4 * N], BF16, name="egr%d_%d" % (b, k), tag="egr", bufs=3, align_bytes=64
                    )
            tr = st["tr"]
            enat = st[("enat", b)]
            nc.tensor.transpose(
                tr[:, 256 * u + 128 * cc : 256 * u + 128 * cc + 128],
                enat[:, k, 2 * h + cc, :].bitcast(F32)[:, 128 * u : 128 * u + 128],
                ident[:],
            )
            if u == 1 and cc == 1:
                egr = st[("egr", b, k)]
                evac(
                    ET_EXIT.get(b, ET_EXIT["all"])[2 * k + h],
                    egr[:].bitcast(F32).rearrange("p (i u) -> p i u", u=2)[:, 256 * h : 256 * h + 256, :],
                    tr[:].rearrange("p (u i) -> p i u", u=2),
                )

        def ht_op(b, v, i):
            u = i // 2
            s = i % 2
            if i == 0:
                st["tr"] = bank("trh%d_%d" % (b, v))
                if v == 0:
                    st[("ht", b)] = work.tile([P, 2, N, 2], BF16, name="ht%d" % b, tag="ht", align_bytes=64)
            tr = st["tr"]
            ha = st[("ha", b)]
            c = 2 * v + s
            nc.tensor.transpose(
                tr[:, 128 * i : 128 * i + 128],
                ha[:, 512 * c : 512 * c + 512].bitcast(F32)[:, 128 * u : 128 * u + 128],
                ident[:],
            )
            if i == 3:
                words = st[("ht", b)][:].rearrange("p u n e -> p (u n e)").bitcast(F32)
                evac(
                    HT_EXIT.get(b, HT_EXIT["all"])[v],
                    words.rearrange("p (u v q s) -> p v u q s", u=2, v=2, s=2)[:, v],
                    tr[:].rearrange("p (u s q) -> p u q s", u=2, s=2),
                )

        def d_op(b, c, k, c2):
            if c == 0 and k == 0 and c2 == 0:
                st["dp"] = bank("dp%d" % b)
            dp = st["dp"]
            enat = st[("enat", b)]
            nc.tensor.matmul(
                dp[:, 16 * c : 16 * c + 16],
                lhsT=enat[:, k, c2, 128 * c : 128 * c + 128],
                rhs=ones[:],
                start=(k == 0 and c2 == 0),
                stop=(k == K - 1 and c2 == 3),
            )
            if c == 3 and k == K - 1 and c2 == 3:
                dsum = work.tile([P, 4], F32, name="dsum%d" % b, tag="dsum")
                nc.scalar.activation(
                    out=dsum[:], in_=dp[:, 0:64].rearrange("p (c n) -> p c n", n=16)[:, :, 0], func=ACT.Copy, bias=2.0
                )
                st[("dsum", b)] = dsum

        def invert_d(b):
            dinv = work.tile([P, 4], F32, name="dinv%d" % b, tag="dinv", bufs=3)
            nc.vector.reciprocal(out=dinv[:], in_=st[("dsum", b)][:])
            st[("dinv", b)] = dinv

        def self_op(b, c, q):
            if q == 0:
                st[("sp", b, c)] = bank("sp%d_%d" % (b, c))
            sp = st[("sp", b, c)]
            ht = st[("ht", b)]
            u = q // 2
            e = q % 2
            nc.tensor.matmul(
                sp[:],
                lhsT=ht[:, u, 128 * c : 128 * c + 128, e],
                rhs=sw_sb[:, u, e, :],
                start=(q == 0),
                stop=(q == 3),
            )
            if q == 3:
                ssb = work.tile([P, F], F32, name="ssb%d_%d" % (b, c), tag="ssb", bufs=8)
                evac(SELF_EXIT.get(b, SELF_EXIT["all"])[c], ssb[:], sp[:])
                st[("ssb", b, c)] = ssb

        def e_transposes(b):
            ops = []
            for k in range(K):
                for h in range(2):
                    for u in range(2):
                        for cc in range(2):
                            ops.append(lambda k=k, h=h, u=u, cc=cc: et_op(b, k, h, u, cc))
            return ops

        def h_transposes(b):
            ops = []
            for v in range(2):
                for i in range(4):
                    ops.append(lambda v=v, i=i: ht_op(b, v, i))
            return ops

        def d_ops(b):
            ops = []
            for c in range(4):
                for k in range(K):
                    for c2 in range(4):
                        ops.append(lambda c=c, k=k, c2=c2: d_op(b, c, k, c2))
            return ops

        def self_ops(b, cs):
            ops = []
            for c in cs:
                for q in range(4):
                    ops.append(lambda c=c, q=q: self_op(b, c, q))
            return ops

        def sigmoid_store(b, c, width):
            y = st[("y", b)]
            nc.scalar.activation(out=y[:, c : c + width, :], in_=y[:, c : c + width, :], func=ACT.Sigmoid)
            nc.sync.dma_start(
                out=out[b].rearrange("(c p) f -> p c f", p=P)[:, c : c + width, :], in_=y[:, c : c + width, :]
            )

        def plain_phase(b):
            mains = self_ops(b, (2, 3) if b < B - 1 else LASTC) if b > 0 else []
            if b + 1 < B:
                mains.extend(self_ops(b + 1, (0, 1) if b + 1 < B - 1 else [c for c in range(4) if c not in LASTC]))
            trs = []
            if b + 1 < B:
                trs.extend(e_transposes(b + 1))
            if b + 2 < B:
                trs.extend(h_transposes(b + 2))
            seq = []
            done = 0
            for i in range(len(mains)):
                seq.append((("mm", i), mains[i]))
                want = min(len(trs), (i + 1) * 3 // 2)
                for j in range(done, want):
                    seq.append((("tr", j), trs[j]))
                done = want
            for j in range(done, len(trs)):
                seq.append((("tr", j), trs[j]))
            if b + 1 < B:
                ds = d_ops(b + 1)
                for j in range(len(ds)):
                    seq.append((("d", j), ds[j]))
            labels = [item[0] for item in seq]
            extras = {}

            def after(label, op):
                key = label if label in labels else labels[-1]
                if key not in extras:
                    extras[key] = []
                extras[key].append(op)

            if b == 0:
                after(QW, lambda: quantise_w())
            if b == B - 1:
                after(("mm", 1), lambda: quantise_x(b, 1))
                after(SG, lambda: sigmoid_store(b - 1, 0, 2))
                after(SG, lambda: sigmoid_store(b - 1, 2, 2))
            if b + 1 < B:
                after(QX1, lambda: quantise_x(b, 1))
                after(RG, lambda: regroup_h(b + 1))
                after(QE0, lambda: quantise_e(b + 1, 0))
                after(QE1, lambda: quantise_e(b + 1, 1))
                after(QH, lambda: quantise_h(b + 1))
            for label, op in seq:
                op()
                for extra in extras.get(label, ()):
                    extra()

        def stage1(b):
            hc = st[("hc", b)]
            hs = st[("hs", b)]
            xgr = work.tile([P, K, 4 * N], BF16, name="xgr%d" % b, tag="xgr", align_bytes=64)
            xc = work.tile([P, K, N], U32, name="xc%d" % b, tag="xc", align_bytes=64)
            xs = work.tile([P, K, N], U8, name="xs%d" % b, tag="xs", align_bytes=64)
            st[("xgr", b)] = xgr
            st[("xc", b)] = xc
            st[("xs", b)] = xs
            for k in range(K):
                ec = st[("ec", b, k)]
                es = st[("es", b, k)]
                for ib in range(4):
                    g = bank("g%d_%d_%d" % (b, k, ib))
                    for t in range(4):
                        nc.tensor.matmul_mx(
                            out=g[:, 128 * t : 128 * t + 128],
                            lhsT=hc[:, 128 * t : 128 * t + 128].bitcast(FP8X4),
                            lhsT_scale=hs[:, 128 * t : 128 * t + 128],
                            rhs=ec[:, 128 * ib : 128 * ib + 128].bitcast(FP8X4),
                            rhs_scale=es[:, 128 * ib : 128 * ib + 128],
                            start=True,
                            stop=True,
                        )
                    evac(
                        G_EXIT.get(b, G_EXIT["all"])[4 * k + ib],
                        xgr[:, k, :].rearrange("p (i t) -> p i t", t=4)[:, 128 * ib : 128 * ib + 128, :],
                        g[:].rearrange("p (t i) -> p i t", t=4),
                    )
                    if k == 1 and ib == QX0:
                        quantise_x(b, 0)

        def quantise_x(b, k):
            nc.vector.quantize_mx(
                out=st[("xc", b)][:, k, :].bitcast(FP8X4), scales=st[("xs", b)][:, k, :], in_=st[("xgr", b)][:, k, :]
            )

        def stage2(b):
            xc = st[("xc", b)]
            xs = st[("xs", b)]
            dinv = st[("dinv", b)]
            if 1 <= b < B - 1:
                sigmoid_store(b - 1, 0, 2)
                sigmoid_store(b - 1, 2, 2)
            y = work.tile([P, 4, F], F32, name="y%d" % b, tag="y", bufs=B)
            st[("y", b)] = y
            for c in range(4):
                if c == 1 and b + 1 < B:
                    invert_d(b + 1)
                widths = TAIL.get(c, (F,)) if b == B - 1 else (F,)
                f0 = 0
                for width in widths:
                    fs = slice(f0, f0 + width)
                    r = bank("r%d_%d_%d" % (b, c, f0))
                    for k in range(K):
                        nc.tensor.matmul_mx(
                            out=r[:, 0:width],
                            lhsT=xc[:, k, 128 * c : 128 * c + 128].bitcast(FP8X4),
                            lhsT_scale=xs[:, k, 128 * c : 128 * c + 128],
                            rhs=w_codes[:, k, fs].bitcast(FP8X4),
                            rhs_scale=w_scales[:, k, fs],
                            start=(k == 0),
                            stop=(k == K - 1),
                        )
                    nc.vector.scalar_tensor_tensor(
                        out=y[:, c, fs],
                        in0=r[:, 0:width],
                        scalar=dinv[:, c : c + 1],
                        in1=st[("ssb", b, c)][:, fs],
                        op0=ALU.mult,
                        op1=ALU.add,
                    )
                    if b == B - 1:
                        nc.scalar.activation(out=y[:, c, fs], in_=y[:, c, fs], func=ACT.Sigmoid)
                        nc.sync.dma_start(out=out[b, 128 * c : 128 * c + 128, fs], in_=y[:, c, fs])
                    f0 += width

        trs = h_transposes(0)
        for op in trs[0:4]:
            op()
        mains = self_ops(0, (0, 1, 2, 3))
        mains = mains[0:2] + mains[4:6] + mains[2:4] + mains[6:]
        for i in range(HP):
            mains[i]()
        for op in trs[4:8]:
            op()
        regroup_h(0)
        quantise_h(0)
        regroup_w()
        trs = e_transposes(0)
        for i in range(HP, 16):
            mains[i]()
            for j in range(max(0, min(16, (i - HS) * 3 // 2)), max(0, min(16, (i + 1 - HS) * 3 // 2))):
                trs[j]()
                if j == 11:
                    quantise_e(0, 0)
        for op in d_ops(0):
            op()
        for op in h_transposes(1):
            op()
        quantise_e(0, 1)
        invert_d(0)
        stage1(0)
        for b in range(B):
            if b + 2 < B:
                load_e(b + 2, 0, 1)
                load_e(b + 2, 1, 1)
            if b + 3 < B:
                load_ha(b + 3)
            plain_phase(b)
            stage2(b)
            if b + 1 < B:
                stage1(b + 1)
